import numpy as np
import ml_dtypes


def mxq(x, axis, fmt="e4m3"):
    dtype, down = {"e4m3": (ml_dtypes.float8_e4m3fn, 7), "e5m2": (ml_dtypes.float8_e5m2, 14)}[fmt]
    v = np.moveaxis(np.asarray(x, np.float32).astype(ml_dtypes.bfloat16).astype(np.float64), axis, -1)
    blocks = v.reshape(v.shape[:-1] + (-1, 32))
    amax = np.abs(blocks).max(-1, keepdims=True)
    byte = np.maximum(np.where(amax > 0, np.frexp(amax)[1] - 1 + 127, 0) - down, 1)
    scale = np.exp2(byte - 127.0)
    codes = (blocks / scale).astype(np.float32).astype(dtype).astype(np.float64)
    return np.moveaxis((codes * scale).reshape(v.shape), -1, axis)


WIDE = False


def mx_kscale(k):
    if not WIDE:
        return np.ones(k)
    levels = np.array([10, -10, 5, -5, 0])
    if k % 512:
        return np.exp2(np.random.permutation(np.resize(levels, k // 32))).repeat(32)
    a = np.empty((k // 512, 16))
    for p in range(k // 512):
        a[p, :8] = np.random.permutation(np.resize(levels, 8))
        for g in range(8):
            far = levels[np.abs(levels - a[p, g]) >= 10]
            a[p, g + 8] = far[np.random.randint(len(far))]
    return np.exp2(a.ravel()).repeat(32)


BF16 = ml_dtypes.bfloat16


def bf(x):
    return np.asarray(x, np.float32).astype(BF16)


def f64(x):
    return np.asarray(x).astype(np.float64)


B, S, D, E = 2, 512, 512, 512
SC = 1.5


def setup_inputs():
    s, t = mx_kscale(D), mx_kscale(E)
    rn = np.random.standard_normal
    qs = np.sqrt(SC / np.sqrt(2.0 * E))
    ws = qs / np.sqrt(2.0 * D)
    return {"x_re": bf(rn((B, S, D)) * s), "x_im": bf(rn((B, S, D)) * s),
            "Wq_re": bf(rn((E, D)) * ws * t[:, None] / s), "Wq_im": bf(rn((E, D)) * ws * t[:, None] / s),
            "bq_re": bf(rn(E) * 0.5 * qs * t), "bq_im": bf(rn(E) * 0.5 * qs * t),
            "Wk_re": bf(rn((E, D)) * ws / t[:, None] / s), "Wk_im": bf(rn((E, D)) * ws / t[:, None] / s),
            "bk_re": bf(rn(E) * 0.5 * qs / t), "bk_im": bf(rn(E) * 0.5 * qs / t)}


def cproj(xr, xi, w_re, w_im, b_re, b_im):
    wr = mxq(f64(w_re), 1, "e4m3").T
    wi = mxq(f64(w_im), 1, "e4m3").T
    y_re = (xr @ wr) - (xi @ wi) + f64(b_re)
    y_im = (xr @ wi) + (xi @ wr) + f64(b_im)
    return y_re, y_im


def reference(x_re, x_im, Wq_re, Wq_im, bq_re, bq_im, Wk_re, Wk_im, bk_re, bk_im):
    xr = mxq(f64(x_re), 2, "e4m3")
    xi = mxq(f64(x_im), 2, "e4m3")
    q_re, q_im = cproj(xr, xi, Wq_re, Wq_im, bq_re, bq_im)
    k_re, k_im = cproj(xr, xi, Wk_re, Wk_im, bk_re, bk_im)
    return ((mxq(q_re, 2, "e4m3") @ mxq(k_re, 2, "e4m3").transpose(0, 2, 1))
            + (mxq(q_im, 2, "e4m3") @ mxq(k_im, 2, "e4m3").transpose(0, 2, 1)))

@@ -1,0 +1,261 @@
+from contextlib import ExitStack
+
+import concourse.mybir as mybir
+from concourse.masks import make_identity
+
+F32 = mybir.dt.float32
+BF16 = mybir.dt.bfloat16
+U32 = mybir.dt.uint32
+U8 = mybir.dt.uint8
+FP8X4 = mybir.dt.float8_e4m3fn_x4
+
+P = 128
+PACK = 4
+BANK = 512
+BATCH = 2
+TOKENS = 512
+FEATURES = 512
+GROUPS = 4
+PIECE = 2 * FEATURES
+SCORE_LAG = 3
+RE = 0
+IM = 1
+
+FLOPS = 8 * 2 * BATCH * TOKENS * FEATURES * FEATURES + 2 * 2 * BATCH * TOKENS * TOKENS * FEATURES
+
+
+def new_mx_operand(pool, name, columns):
+    codes = pool.tile([P, columns], U32, name=name + "_codes", align_bytes=64)
+    scales = pool.tile([P, columns], U8, name=name + "_scales", align_bytes=64)
+    return {"codes": codes, "scales": scales}
+
+
+def quantise(nc, operand, first, values):
+    columns = slice(first, first + values.shape[1] // PACK)
+    nc.vector.quantize_mx(
+        out=operand["codes"][:, columns].bitcast(FP8X4),
+        scales=operand["scales"][:, columns],
+        in_=values,
+    )
+
+
+def mx_pass(nc, acc, stationary, s_first, moving, m_first, start, stop):
+    s_columns = slice(s_first, s_first + P)
+    m_columns = slice(m_first, m_first + acc.shape[1])
+    nc.tensor.matmul_mx(
+        out=acc,
+        lhsT=stationary["codes"][:, s_columns].bitcast(FP8X4),
+        lhsT_scale=stationary["scales"][:, s_columns],
+        rhs=moving["codes"][:, m_columns].bitcast(FP8X4),
+        rhs_scale=moving["scales"][:, m_columns],
+        start=start,
+        stop=stop,
+    )
+
+
+def tile_teleportationattention_pa_kernel(
+    tc, x_re, x_im, Wq_re, Wq_im, bq_re, bq_im, Wk_re, Wk_im, bk_re, bk_im, out
+):
+    nc = tc.nc
+    with ExitStack() as ctx:
+        keep = ctx.enter_context(tc.tile_pool(name="keep", bufs=1))
+        work = ctx.enter_context(tc.tile_pool(name="work", bufs=4))
+        psum = ctx.enter_context(tc.psum_pool(name="psum", bufs=8))
+        ctx.enter_context(tc.manual_schedule())
+
+        ident = keep.tile([P, P], F32, name="ident")
+        make_identity(nc, ident[:])
+
+        bias_slots = keep.tile([P, 4, 16], BF16, name="bias_slots")
+        bias = {}
+        for n, (kind, part, vector) in enumerate(
+            (("q", RE, bq_re), ("q", IM, bq_im), ("k", RE, bk_re), ("k", IM, bk_im))
+        ):
+            bias[kind, part] = bias_slots[:, n, 0:PACK]
+            nc.scalar.dma_start(out=bias[kind, part], in_=vector.rearrange("(r t) -> r t", t=PACK))
+
+        def load(name, matrix, first_group, groups):
+            raw = keep.tile([P, groups * FEATURES], BF16, name=name)
+            by_partition = matrix.rearrange("(r j) d -> r (j d)", j=GROUPS)
+            first = first_group * FEATURES
+            nc.sync.dma_start(out=raw[:], in_=by_partition[:, first : first + groups * FEATURES])
+            return raw
+
+        raw_w = {}
+        raw_x = {}
+
+        def load_weights(kind, w_re, w_im):
+            for part, name, matrix in ((IM, "im", w_im), (RE, "re", w_re)):
+                whole = load("raw_w" + kind + "_" + name, matrix, 0, GROUPS)
+                raw_w[kind, part] = [whole[:, 0:PIECE], whole[:, PIECE : 2 * PIECE]]
+
+        def load_tokens(b):
+            raw_x[b, RE] = []
+            raw_x[b, IM] = []
+            for half in range(2):
+                tail = str(b) + "_" + str(half)
+                raw_x[b, RE].append(load("raw_x_re" + tail, x_re[b, :, :], 2 * half, 2)[:])
+                raw_x[b, IM].append(load("raw_x_im" + tail, x_im[b, :, :], 2 * half, 2)[:])
+
+        load_weights("q", Wq_re, Wq_im)
+        load_tokens(0)
+        load_weights("k", Wk_re, Wk_im)
+        load_tokens(1)
+
+        weight = {}
+        for kind in ("k", "q"):
+            for name in ("re", "im", "im_neg"):
+                weight[kind, name] = new_mx_operand(keep, "w" + kind + "_" + name, FEATURES)
+        tokens = new_mx_operand(keep, "x", BATCH * 2 * TOKENS)
+        keys = new_mx_operand(keep, "k", BATCH * 2 * TOKENS)
+        queries = new_mx_operand(keep, "q", BATCH * 2 * TOKENS)
+
+        def part_major_column(b, part, j):
+            return ((b * 2 + part) * GROUPS + j) * P
+
+        def group_major_column(b, part, j):
+            return ((b * GROUPS + j) * 2 + part) * P
+
+        def features_to_partitions(piece):
+            raw_pairs = piece.bitcast(F32)
+            grouped = work.tile([P, PIECE], BF16, tag="grouped_in", bufs=8, align_bytes=64)
+            bank = psum.tile([P, BANK], F32, tag="bank")
+            for s in range(4):
+                columns = slice(s * P, (s + 1) * P)
+                first = (s // 2) * 2 * P + s % 2
+                nc.tensor.transpose(bank[:, columns], raw_pairs[:, first : first + 2 * P - 1 : 2], ident[:])
+            nc.scalar.copy(
+                out=grouped[:].bitcast(F32).rearrange("p (j r u) -> p j r u", j=2, u=2),
+                in_=bank[:].rearrange("p (j u r) -> p j r u", j=2, u=2),
+            )
+            return grouped
+
+        def transpose_weights(kind):
+            return {part: [features_to_partitions(piece) for piece in raw_w[kind, part]] for part in (IM, RE)}
+
+        def quantise_weights(kind, grouped):
+            for half in range(2):
+                first = half * PIECE // PACK
+                negated = work.tile([P, PIECE], BF16, tag="negated", align_bytes=64)
+                nc.vector.tensor_scalar_mul(out=negated[:], in0=grouped[IM][half][:], scalar1=-1.0)
+                quantise(nc, weight[kind, "im"], first, grouped[IM][half][:])
+                quantise(nc, weight[kind, "im_neg"], first, negated[:])
+            for half in range(2):
+                quantise(nc, weight[kind, "re"], half * PIECE // PACK, grouped[RE][half][:])
+
+        def transpose_tokens(b):
+            return [{part: features_to_partitions(raw_x[b, part][half]) for part in (RE, IM)} for half in range(2)]
+
+        def quantise_tokens(b, grouped):
+            for half in range(2):
+                for part in (RE, IM):
+                    quantise(nc, tokens, part_major_column(b, part, 2 * half), grouped[half][part][:])
+
+        def project(acc, kind, part, t, b, j):
+            w_of_x_re, w_of_x_im = (("re", "im_neg"), ("im", "re"))[part]
+            mx_pass(nc, acc, weight[kind, w_of_x_re], t * P, tokens, part_major_column(b, RE, j), True, False)
+            mx_pass(nc, acc, weight[kind, w_of_x_im], t * P, tokens, part_major_column(b, IM, j), False, True)
+
+        def project_queries(b, j):
+            grouped = work.tile([P, 2 * BANK], BF16, tag="grouped_q", align_bytes=64)
+            for part in (RE, IM):
+                bank = psum.tile([P, BANK], F32, tag="bank")
+                for t in range(PACK):
+                    project(bank[:, t * P : (t + 1) * P], "q", part, t, b, j)
+                nc.vector.tensor_tensor(
+                    out=grouped[:, part * BANK : (part + 1) * BANK].rearrange("p (n t) -> p n t", t=PACK),
+                    in0=bank[:].rearrange("p (t n) -> p n t", t=PACK),
+                    in1=bias["q", part].unsqueeze(1).to_broadcast([P, P, PACK]),
+                    op=mybir.AluOpType.add,
+                )
+            return grouped
+
+        def quantise_queries(b, j, grouped):
+            quantise(nc, queries, group_major_column(b, RE, j), grouped[:])
+
+        def project_keys(b, part):
+            planes = work.tile([P, PACK * TOKENS], BF16, tag="planes", bufs=2)
+            for t in range(PACK):
+                bank = psum.tile([P, BANK], F32, tag="bank")
+                project(bank[:], "k", part, t, b, 0)
+                nc.scalar.activation(
+                    out=planes[:, t * TOKENS : (t + 1) * TOKENS],
+                    in_=bank[:],
+                    func=mybir.ActivationFunctionType.Identity,
+                    bias=bias["k", part][:, t : t + 1],
+                    scale=1.0,
+                )
+            return planes
+
+        def interleave_keys(planes):
+            grouped = work.tile([P, PACK * TOKENS], BF16, tag="grouped_k", bufs=2, align_bytes=64)
+            nc.vector.tensor_copy(
+                out=grouped[:].rearrange("p (c i t) -> p c t i", i=4, t=PACK),
+                in_=planes[:].rearrange("p (t c i) -> p c t i", i=4, t=PACK),
+            )
+            return grouped
+
+        def quantise_keys(b, part, grouped):
+            quantise(nc, keys, part_major_column(b, part, 0), grouped[:])
+
+        def score_rows(b, j):
+            acc = psum.tile([P, BANK], F32, tag="bank")
+            for part in (RE, IM):
+                mx_pass(
+                    nc,
+                    acc[:],
+                    queries,
+                    group_major_column(b, part, j),
+                    keys,
+                    part_major_column(b, part, 0),
+                    part == RE,
+                    part == IM,
+                )
+            rows = work.tile([P, TOKENS], F32, tag="rows")
+            nc.scalar.copy(
+                out=rows[:].rearrange("p (r g) -> p r g", g=GROUPS),
+                in_=acc[:].rearrange("p (g r) -> p r g", g=GROUPS),
+            )
+            nc.sync.dma_start(
+                out=out[b, :, :].rearrange("(r j) k -> r j k", j=GROUPS)[:, j, :], in_=rows[:]
+            )
+
+
+        quantise_weights("q", transpose_weights("q"))
+        quantise_tokens(0, transpose_tokens(0))
+        q_values = {}
+        for j in range(GROUPS):
+            q_values[j] = project_queries(0, j)
+            if j == 0:
+                wk_grouped = transpose_weights("k")
+            if j == 1:
+                x1_grouped = transpose_tokens(1)
+            if j > 0:
+                quantise_queries(0, j - 1, q_values[j - 1])
+            if j == 1:
+                quantise_weights("k", wk_grouped)
+            if j == 2:
+                quantise_tokens(1, x1_grouped)
+        quantise_queries(0, GROUPS - 1, q_values[GROUPS - 1])
+
+        units = [(b, part) for b in range(BATCH) for part in (RE, IM)]
+        k_planes = {}
+        k_values = {}
+        for n in range(len(units) + 2):
+            if n < len(units):
+                k_planes[n] = project_keys(units[n][0], units[n][1])
+            if 1 <= n <= len(units):
+                k_values[n - 1] = interleave_keys(k_planes[n - 1])
+            if n >= 2:
+                quantise_keys(units[n - 2][0], units[n - 2][1], k_values[n - 2])
+                if units[n - 2] == (0, IM):
+                    for j in range(GROUPS):
+                        score_rows(0, j)
+
+        for j in range(GROUPS + SCORE_LAG):
+            if j < GROUPS:
+                q_values[j] = project_queries(1, j)
+            if 1 <= j <= GROUPS:
+                quantise_queries(1, j - 1, q_values[j - 1])
+            if j >= SCORE_LAG:
+                score_rows(1, j - SCORE_LAG)

@@ -18,6 +18,7 @@ FEATURES = 512
 GROUPS = 4
 PIECE = 2 * FEATURES
 SCORE_LAG = 3
+WARM_UP = 4
 RE = 0
 IM = 1
 
@@ -66,39 +67,46 @@ def tile_teleportationattention_pa_kernel(
         ident = keep.tile([P, P], F32, name="ident")
         make_identity(nc, ident[:])
 
+        zeros = keep.tile([P, BANK], BF16, name="zeros")
+        nc.vector.memset(zeros[:], 0.0)
+        warm = psum.tile([P, BANK], F32, tag="bank")
+        for n in range(WARM_UP):
+            nc.tensor.matmul(warm[:], lhsT=zeros[:, 0:P], rhs=zeros[:], start=True, stop=True)
+
         bias_slots = keep.tile([P, 4, 16], BF16, name="bias_slots")
         bias = {}
-        for n, (kind, part, vector) in enumerate(
-            (("q", RE, bq_re), ("q", IM, bq_im), ("k", RE, bk_re), ("k", IM, bk_im))
-        ):
-            bias[kind, part] = bias_slots[:, n, 0:PACK]
-            nc.scalar.dma_start(out=bias[kind, part], in_=vector.rearrange("(r t) -> r t", t=PACK))
 
-        def load(name, matrix, first_group, groups):
-            raw = keep.tile([P, groups * FEATURES], BF16, name=name)
-            by_partition = matrix.rearrange("(r j) d -> r (j d)", j=GROUPS)
-            first = first_group * FEATURES
-            nc.sync.dma_start(out=raw[:], in_=by_partition[:, first : first + groups * FEATURES])
-            return raw
+        def load(name, rows):
+            raw = keep.tile([P, PIECE], BF16, name=name)
+            nc.sync.dma_start(out=raw[:], in_=rows)
+            return raw[:]
 
         raw_w = {}
         raw_x = {}
 
         def load_weights(kind, w_re, w_im):
             for part, name, matrix in ((IM, "im", w_im), (RE, "re", w_re)):
-                whole = load("raw_w" + kind + "_" + name, matrix, 0, GROUPS)
-                raw_w[kind, part] = [whole[:, 0:PIECE], whole[:, PIECE : 2 * PIECE]]
+                rows = matrix.rearrange("(r j) d -> r (j d)", j=GROUPS)
+                raw_w[kind, part] = [
+                    load("raw_w" + kind + "_" + name + str(c), rows[:, c * PIECE : (c + 1) * PIECE]) for c in range(2)
+                ]
 
         def load_tokens(b):
             raw_x[b, RE] = []
             raw_x[b, IM] = []
             for half in range(2):
                 tail = str(b) + "_" + str(half)
-                raw_x[b, RE].append(load("raw_x_re" + tail, x_re[b, :, :], 2 * half, 2)[:])
-                raw_x[b, IM].append(load("raw_x_im" + tail, x_im[b, :, :], 2 * half, 2)[:])
+                for part, name, matrix in ((RE, "re", x_re), (IM, "im", x_im)):
+                    rows = matrix[b, half * 256 : (half + 1) * 256, :].rearrange("(r i) d -> r (i d)", i=2)
+                    raw_x[b, part].append(load("raw_x_" + name + tail, rows))
 
         load_weights("q", Wq_re, Wq_im)
         load_tokens(0)
+        for n, (kind, part, vector) in enumerate(
+            (("q", RE, bq_re), ("q", IM, bq_im), ("k", RE, bk_re), ("k", IM, bk_im))
+        ):
+            bias[kind, part] = bias_slots[:, n, 0:PACK]
+            nc.sync.dma_start(out=bias[kind, part], in_=vector.rearrange("(r t) -> r t", t=PACK))
         load_weights("k", Wk_re, Wk_im)
         load_tokens(1)
 
@@ -213,11 +221,11 @@ def tile_teleportationattention_pa_kernel(
                 )
             rows = work.tile([P, TOKENS], F32, tag="rows")
             nc.scalar.copy(
-                out=rows[:].rearrange("p (r g) -> p r g", g=GROUPS),
-                in_=acc[:].rearrange("p (g r) -> p r g", g=GROUPS),
+                out=rows[:].rearrange("p (h r i) -> p h r i", h=2, i=2),
+                in_=acc[:].rearrange("p (h i r) -> p h r i", h=2, i=2),
             )
             nc.sync.dma_start(
-                out=out[b, :, :].rearrange("(r j) k -> r j k", j=GROUPS)[:, j, :], in_=rows[:]
+                out=out[b, :, :].rearrange("(h r i) k -> h r i k", h=2, i=2)[j // 2, :, j % 2, :], in_=rows[:]
             )
 
 

@@ -17,7 +17,6 @@ TOKENS = 512
 FEATURES = 512
 GROUPS = 4
 PIECE = 2 * FEATURES
-SCORE_LAG = 3
 WARM_UP = 4
 RE = 0
 IM = 1
@@ -85,11 +84,14 @@ def tile_teleportationattention_pa_kernel(
         raw_x = {}
 
         def load_weights(kind, w_re, w_im):
-            for part, name, matrix in ((IM, "im", w_im), (RE, "re", w_re)):
-                rows = matrix.rearrange("(r j) d -> r (j d)", j=GROUPS)
-                raw_w[kind, part] = [
-                    load("raw_w" + kind + "_" + name + str(c), rows[:, c * PIECE : (c + 1) * PIECE]) for c in range(2)
-                ]
+            raw_w[kind, RE] = []
+            raw_w[kind, IM] = []
+            for c in range(2):
+                for part, name, matrix in ((IM, "im", w_im), (RE, "re", w_re)):
+                    rows = matrix.rearrange("(r j) d -> r (j d)", j=GROUPS)
+                    raw_w[kind, part].append(
+                        load("raw_w" + kind + "_" + name + str(c), rows[:, c * PIECE : (c + 1) * PIECE])
+                    )
 
         def load_tokens(b):
             raw_x[b, RE] = []
@@ -138,48 +140,61 @@ def tile_teleportationattention_pa_kernel(
             )
             return grouped
 
+        w_grouped = {}
+        x_grouped = {}
+
         def transpose_weights(kind):
-            return {part: [features_to_partitions(piece) for piece in raw_w[kind, part]] for part in (IM, RE)}
+            for c in range(2):
+                for part in (IM, RE):
+                    w_grouped[kind, part, c] = features_to_partitions(raw_w[kind, part][c])
 
-        def quantise_weights(kind, grouped):
-            for half in range(2):
-                first = half * PIECE // PACK
-                negated = work.tile([P, PIECE], BF16, tag="negated", align_bytes=64)
-                nc.vector.tensor_scalar_mul(out=negated[:], in0=grouped[IM][half][:], scalar1=-1.0)
-                quantise(nc, weight[kind, "im"], first, grouped[IM][half][:])
-                quantise(nc, weight[kind, "im_neg"], first, negated[:])
-            for half in range(2):
-                quantise(nc, weight[kind, "re"], half * PIECE // PACK, grouped[RE][half][:])
+        def negate_weight(kind, c):
+            negated = work.tile([P, PIECE], BF16, tag="negated", align_bytes=64)
+            nc.vector.tensor_scalar_mul(out=negated[:], in0=w_grouped[kind, IM, c][:], scalar1=-1.0)
+            w_grouped[kind, "neg", c] = negated
 
-        def transpose_tokens(b):
-            return [{part: features_to_partitions(raw_x[b, part][half]) for part in (RE, IM)} for half in range(2)]
+        def quantise_weight(kind, name, c):
+            source = {"re": RE, "im": IM, "im_neg": "neg"}[name]
+            quantise(nc, weight[kind, name], c * PIECE // PACK, w_grouped[kind, source, c][:])
 
-        def quantise_tokens(b, grouped):
-            for half in range(2):
-                for part in (RE, IM):
-                    quantise(nc, tokens, part_major_column(b, part, 2 * half), grouped[half][part][:])
+        def transpose_tokens(b, half):
+            for part in (RE, IM):
+                x_grouped[b, part, half] = features_to_partitions(raw_x[b, part][half])
+
+        def quantise_tokens(b, half):
+            for part in (RE, IM):
+                quantise(nc, tokens, part_major_column(b, part, 2 * half), x_grouped[b, part, half][:])
 
         def project(acc, kind, part, t, b, j):
             w_of_x_re, w_of_x_im = (("re", "im_neg"), ("im", "re"))[part]
             mx_pass(nc, acc, weight[kind, w_of_x_re], t * P, tokens, part_major_column(b, RE, j), True, False)
             mx_pass(nc, acc, weight[kind, w_of_x_im], t * P, tokens, part_major_column(b, IM, j), False, True)
 
+        q_banks = {}
+        q_values = {}
+
         def project_queries(b, j):
-            grouped = work.tile([P, 2 * BANK], BF16, tag="grouped_q", align_bytes=64)
             for part in (RE, IM):
                 bank = psum.tile([P, BANK], F32, tag="bank")
                 for t in range(PACK):
                     project(bank[:, t * P : (t + 1) * P], "q", part, t, b, j)
-                nc.vector.tensor_tensor(
-                    out=grouped[:, part * BANK : (part + 1) * BANK].rearrange("p (n t) -> p n t", t=PACK),
-                    in0=bank[:].rearrange("p (t n) -> p n t", t=PACK),
-                    in1=bias["q", part].unsqueeze(1).to_broadcast([P, P, PACK]),
-                    op=mybir.AluOpType.add,
-                )
-            return grouped
+                q_banks[b, j, part] = bank
 
-        def quantise_queries(b, j, grouped):
-            quantise(nc, queries, group_major_column(b, RE, j), grouped[:])
+        def add_query_bias(b, j, part):
+            if part == RE:
+                q_values[b, j] = work.tile([P, 2 * BANK], BF16, tag="grouped_q", name="grouped_q", bufs=8, align_bytes=64)
+            nc.vector.tensor_tensor(
+                out=q_values[b, j][:, part * BANK : (part + 1) * BANK].rearrange("p (n t) -> p n t", t=PACK),
+                in0=q_banks[b, j, part][:].rearrange("p (t n) -> p n t", t=PACK),
+                in1=bias["q", part].unsqueeze(1).to_broadcast([P, P, PACK]),
+                op=mybir.AluOpType.add,
+            )
+
+        def quantise_queries(b, j):
+            quantise(nc, queries, group_major_column(b, RE, j), q_values[b, j][:])
+
+        k_planes = {}
+        k_values = {}
 
         def project_keys(b, part):
             planes = work.tile([P, PACK * TOKENS], BF16, tag="planes", bufs=2)
@@ -193,77 +208,130 @@ def tile_teleportationattention_pa_kernel(
                     bias=bias["k", part][:, t : t + 1],
                     scale=1.0,
                 )
-            return planes
+            k_planes[b, part] = planes
 
-        def interleave_keys(planes):
+        def interleave_keys(b, part):
             grouped = work.tile([P, PACK * TOKENS], BF16, tag="grouped_k", bufs=2, align_bytes=64)
             nc.vector.tensor_copy(
                 out=grouped[:].rearrange("p (c i t) -> p c t i", i=4, t=PACK),
-                in_=planes[:].rearrange("p (t c i) -> p c t i", i=4, t=PACK),
+                in_=k_planes[b, part][:].rearrange("p (t c i) -> p c t i", i=4, t=PACK),
             )
-            return grouped
+            k_values[b, part] = grouped
 
-        def quantise_keys(b, part, grouped):
-            quantise(nc, keys, part_major_column(b, part, 0), grouped[:])
+        def quantise_keys(b, part):
+            quantise(nc, keys, part_major_column(b, part, 0), k_values[b, part][:])
 
-        def score_rows(b, j):
-            acc = psum.tile([P, BANK], F32, tag="bank")
+        def score_passes(acc, b, j, first_key):
             for part in (RE, IM):
                 mx_pass(
                     nc,
-                    acc[:],
+                    acc,
                     queries,
                     group_major_column(b, part, j),
                     keys,
-                    part_major_column(b, part, 0),
+                    part_major_column(b, part, 0) + first_key,
                     part == RE,
                     part == IM,
                 )
+
+        def rows_of_group(b, j):
+            return out[b, :, :].rearrange("(h r i) k -> h r i k", h=2, i=2)[j // 2, :, j % 2, :]
+
+        def score_rows(b, j):
+            acc = psum.tile([P, BANK], F32, tag="bank")
+            score_passes(acc[:], b, j, 0)
             rows = work.tile([P, TOKENS], F32, tag="rows")
             nc.scalar.copy(
                 out=rows[:].rearrange("p (h r i) -> p h r i", h=2, i=2),
                 in_=acc[:].rearrange("p (h i r) -> p h r i", h=2, i=2),
             )
-            nc.sync.dma_start(
-                out=out[b, :, :].rearrange("(h r i) k -> h r i k", h=2, i=2)[j // 2, :, j % 2, :], in_=rows[:]
-            )
+            nc.sync.dma_start(out=rows_of_group(b, j), in_=rows[:])
 
+        def last_score_rows(b, j):
+            for half, copy, queue in ((0, nc.scalar.copy, nc.scalar), (1, nc.vector.tensor_copy, nc.sync)):
+                acc = psum.tile([P, BANK], F32, tag="bank")
+                score_passes(acc[:, 0 : 2 * P], b, j, half * 2 * P)
+                rows = work.tile([P, 2 * P], F32, tag="half_rows")
+                copy(
+                    out=rows[:].rearrange("p (r i) -> p r i", i=2),
+                    in_=acc[:, 0 : 2 * P].rearrange("p (i r) -> p r i", i=2),
+                )
+                queue.dma_start(out=rows_of_group(b, j)[:, half * 2 * P : (half + 1) * 2 * P], in_=rows[:])
 
-        quantise_weights("q", transpose_weights("q"))
-        quantise_tokens(0, transpose_tokens(0))
-        q_values = {}
-        for j in range(GROUPS):
-            q_values[j] = project_queries(0, j)
-            if j == 0:
-                wk_grouped = transpose_weights("k")
-            if j == 1:
-                x1_grouped = transpose_tokens(1)
-            if j > 0:
-                quantise_queries(0, j - 1, q_values[j - 1])
-            if j == 1:
-                quantise_weights("k", wk_grouped)
-            if j == 2:
-                quantise_tokens(1, x1_grouped)
-        quantise_queries(0, GROUPS - 1, q_values[GROUPS - 1])
+        transpose_weights("q")
+        transpose_tokens(0, 0)
+        transpose_tokens(0, 1)
+        for c in range(2):
+            negate_weight("q", c)
+            if c == 0:
+                quantise_weight("q", "im", c)
+            quantise_weight("q", "re", c)
+            quantise_weight("q", "im_neg", c)
+        quantise_tokens(0, 0)
+        quantise_weight("q", "im", 1)
+        quantise_tokens(0, 1)
 
-        units = [(b, part) for b in range(BATCH) for part in (RE, IM)]
-        k_planes = {}
-        k_values = {}
-        for n in range(len(units) + 2):
-            if n < len(units):
-                k_planes[n] = project_keys(units[n][0], units[n][1])
-            if 1 <= n <= len(units):
-                k_values[n - 1] = interleave_keys(k_planes[n - 1])
-            if n >= 2:
-                quantise_keys(units[n - 2][0], units[n - 2][1], k_values[n - 2])
-                if units[n - 2] == (0, IM):
-                    for j in range(GROUPS):
-                        score_rows(0, j)
-
-        for j in range(GROUPS + SCORE_LAG):
-            if j < GROUPS:
-                q_values[j] = project_queries(1, j)
-            if 1 <= j <= GROUPS:
-                quantise_queries(1, j - 1, q_values[j - 1])
-            if j >= SCORE_LAG:
-                score_rows(1, j - SCORE_LAG)
+        project_queries(0, 0)
+        transpose_weights("k")
+        project_queries(0, 1)
+        add_query_bias(0, 0, RE)
+        add_query_bias(0, 0, IM)
+        for c in range(2):
+            negate_weight("k", c)
+            quantise_weight("k", "re", c)
+            quantise_weight("k", "im_neg", c)
+            if c == 0:
+                project_queries(0, 2)
+                add_query_bias(0, 1, RE)
+                add_query_bias(0, 1, IM)
+        project_keys(0, RE)
+        add_query_bias(0, 2, RE)
+        add_query_bias(0, 2, IM)
+        quantise_weight("k", "im", 0)
+        quantise_weight("k", "im", 1)
+        transpose_tokens(1, 0)
+        project_keys(0, IM)
+        quantise_queries(0, 0)
+        quantise_queries(0, 1)
+        interleave_keys(0, RE)
+        project_queries(0, 3)
+        quantise_tokens(1, 0)
+        quantise_keys(0, RE)
+        transpose_tokens(1, 1)
+        add_query_bias(0, 3, RE)
+        add_query_bias(0, 3, IM)
+        project_queries(1, 0)
+        interleave_keys(0, IM)
+        quantise_tokens(1, 1)
+        quantise_queries(0, 2)
+        project_keys(1, RE)
+        quantise_keys(0, IM)
+        add_query_bias(1, 0, RE)
+        add_query_bias(1, 0, IM)
+        quantise_queries(0, 3)
+        project_queries(1, 1)
+        score_rows(0, 0)
+        project_keys(1, IM)
+        interleave_keys(1, RE)
+        add_query_bias(1, 1, RE)
+        add_query_bias(1, 1, IM)
+        quantise_keys(1, RE)
+        quantise_queries(1, 0)
+        project_queries(1, 2)
+        score_rows(0, 1)
+        score_rows(0, 2)
+        add_query_bias(1, 2, RE)
+        interleave_keys(1, IM)
+        add_query_bias(1, 2, IM)
+        quantise_keys(1, IM)
+        quantise_queries(1, 1)
+        project_queries(1, 3)
+        score_rows(0, 3)
+        add_query_bias(1, 3, RE)
+        quantise_queries(1, 2)
+        add_query_bias(1, 3, IM)
+        score_rows(1, 0)
+        score_rows(1, 1)
+        quantise_queries(1, 3)
+        score_rows(1, 2)
+        last_score_rows(1, 3)

@@ -126,14 +126,23 @@ def tile_teleportationattention_pa_kernel(
         def group_major_column(b, part, j):
             return ((b * GROUPS + j) * 2 + part) * P
 
-        def features_to_partitions(piece):
+        def split_pairs(piece, copy):
+            split = work.tile([P, PIECE], BF16, tag="split", bufs=8, align_bytes=64)
+            copy(
+                out=split[:].bitcast(F32).rearrange("q (j u p) -> q j u p", j=2, u=2),
+                in_=piece.bitcast(F32).rearrange("q (j p u) -> q j u p", j=2, u=2),
+            )
+            return split[:]
+
+        def features_to_partitions(piece, is_split=False):
             raw_pairs = piece.bitcast(F32)
             grouped = work.tile([P, PIECE], BF16, tag="grouped_in", bufs=8, align_bytes=64)
             bank = psum.tile([P, BANK], F32, tag="bank")
             for s in range(4):
                 columns = slice(s * P, (s + 1) * P)
                 first = (s // 2) * 2 * P + s % 2
-                nc.tensor.transpose(bank[:, columns], raw_pairs[:, first : first + 2 * P - 1 : 2], ident[:])
+                words = columns if is_split else slice(first, first + 2 * P - 1, 2)
+                nc.tensor.transpose(bank[:, columns], raw_pairs[:, words], ident[:])
             nc.scalar.copy(
                 out=grouped[:].bitcast(F32).rearrange("p (j r u) -> p j r u", j=2, u=2),
                 in_=bank[:].rearrange("p (j u r) -> p j r u", j=2, u=2),
@@ -146,7 +155,7 @@ def tile_teleportationattention_pa_kernel(
         def transpose_weights(kind):
             for c in range(2):
                 for part in (IM, RE):
-                    w_grouped[kind, part, c] = features_to_partitions(raw_w[kind, part][c])
+                    w_grouped[kind, part, c] = features_to_partitions(raw_w[kind, part][c], kind == "k")
 
         def negate_weight(kind, c):
             negated = work.tile([P, PIECE], BF16, tag="negated", align_bytes=64)
@@ -159,7 +168,7 @@ def tile_teleportationattention_pa_kernel(
 
         def transpose_tokens(b, half):
             for part in (RE, IM):
-                x_grouped[b, part, half] = features_to_partitions(raw_x[b, part][half])
+                x_grouped[b, part, half] = features_to_partitions(raw_x[b, part][half], b == 1)
 
         def quantise_tokens(b, half):
             for part in (RE, IM):
@@ -271,8 +280,14 @@ def tile_teleportationattention_pa_kernel(
         quantise_weight("q", "im", 1)
         quantise_tokens(0, 1)
 
+        for c in range(2):
+            for part in (IM, RE):
+                raw_w["k", part][c] = split_pairs(raw_w["k", part][c], nc.vector.tensor_copy)
         project_queries(0, 0)
         transpose_weights("k")
+        for half in range(2):
+            for part in (RE, IM):
+                raw_x[1, part][half] = split_pairs(raw_x[1, part][half], nc.scalar.copy)
         project_queries(0, 1)
         add_query_bias(0, 0, RE)
         add_query_bias(0, 0, IM)

@@ -69,8 +69,12 @@ def tile_teleportationattention_pa_kernel(
         zeros = keep.tile([P, BANK], BF16, name="zeros")
         nc.vector.memset(zeros[:], 0.0)
         warm = psum.tile([P, BANK], F32, tag="bank")
-        for n in range(WARM_UP):
-            nc.tensor.matmul(warm[:], lhsT=zeros[:, 0:P], rhs=zeros[:], start=True, stop=True)
+
+        def keep_warm(count):
+            for n in range(count):
+                nc.tensor.matmul(warm[:], lhsT=zeros[:, 0:P], rhs=zeros[:], start=True, stop=True)
+
+        keep_warm(WARM_UP)
 
         bias_slots = keep.tile([P, 4, 16], BF16, name="bias_slots")
         bias = {}
@@ -152,10 +156,9 @@ def tile_teleportationattention_pa_kernel(
         w_grouped = {}
         x_grouped = {}
 
-        def transpose_weights(kind):
-            for c in range(2):
-                for part in (IM, RE):
-                    w_grouped[kind, part, c] = features_to_partitions(raw_w[kind, part][c], kind == "k")
+        def transpose_weight(kind, c):
+            for part in (IM, RE):
+                w_grouped[kind, part, c] = features_to_partitions(raw_w[kind, part][c], kind == "k")
 
         def negate_weight(kind, c):
             negated = work.tile([P, PIECE], BF16, tag="negated", align_bytes=64)
@@ -267,8 +270,11 @@ def tile_teleportationattention_pa_kernel(
                 )
                 queue.dma_start(out=rows_of_group(b, j)[:, half * 2 * P : (half + 1) * 2 * P], in_=rows[:])
 
-        transpose_weights("q")
+        for c in range(2):
+            transpose_weight("q", c)
+            keep_warm(1)
         transpose_tokens(0, 0)
+        keep_warm(1)
         transpose_tokens(0, 1)
         for c in range(2):
             negate_weight("q", c)
@@ -284,7 +290,8 @@ def tile_teleportationattention_pa_kernel(
             for part in (IM, RE):
                 raw_w["k", part][c] = split_pairs(raw_w["k", part][c], nc.vector.tensor_copy)
         project_queries(0, 0)
-        transpose_weights("k")
+        transpose_weight("k", 0)
+        transpose_weight("k", 1)
         for half in range(2):
             for part in (RE, IM):
                 raw_x[1, part][half] = split_pairs(raw_x[1, part][half], nc.scalar.copy)

@@ -252,7 +252,7 @@ def tile_teleportationattention_pa_kernel(
         def score_rows(b, j):
             acc = psum.tile([P, BANK], F32, tag="bank")
             score_passes(acc[:], b, j, 0)
-            rows = work.tile([P, TOKENS], F32, tag="rows")
+            rows = work.tile([P, TOKENS], F32, tag="rows", bufs=8)
             nc.scalar.copy(
                 out=rows[:].rearrange("p (h r i) -> p h r i", h=2, i=2),
                 in_=acc[:].rearrange("p (h i r) -> p h r i", h=2, i=2),
@@ -284,11 +284,11 @@ def tile_teleportationattention_pa_kernel(
             quantise_weight("q", "im_neg", c)
         quantise_tokens(0, 0)
         quantise_weight("q", "im", 1)
-        quantise_tokens(0, 1)
 
         for c in range(2):
             for part in (IM, RE):
                 raw_w["k", part][c] = split_pairs(raw_w["k", part][c], nc.vector.tensor_copy)
+        quantise_tokens(0, 1)
         project_queries(0, 0)
         transpose_weight("k", 0)
         transpose_weight("k", 1)
@@ -307,46 +307,46 @@ def tile_teleportationattention_pa_kernel(
                 add_query_bias(0, 1, RE)
                 add_query_bias(0, 1, IM)
         project_keys(0, RE)
-        add_query_bias(0, 2, RE)
-        add_query_bias(0, 2, IM)
         quantise_weight("k", "im", 0)
         quantise_weight("k", "im", 1)
-        transpose_tokens(1, 0)
-        project_keys(0, IM)
+        add_query_bias(0, 2, RE)
+        add_query_bias(0, 2, IM)
         quantise_queries(0, 0)
         quantise_queries(0, 1)
-        interleave_keys(0, RE)
-        project_queries(0, 3)
-        quantise_tokens(1, 0)
-        quantise_keys(0, RE)
+        quantise_queries(0, 2)
+        transpose_tokens(1, 0)
         transpose_tokens(1, 1)
+        project_keys(0, IM)
+        quantise_tokens(1, 0)
+        project_queries(0, 3)
+        interleave_keys(0, RE)
+        quantise_tokens(1, 1)
         add_query_bias(0, 3, RE)
         add_query_bias(0, 3, IM)
-        project_queries(1, 0)
-        interleave_keys(0, IM)
-        quantise_tokens(1, 1)
-        quantise_queries(0, 2)
         project_keys(1, RE)
-        quantise_keys(0, IM)
-        add_query_bias(1, 0, RE)
-        add_query_bias(1, 0, IM)
+        quantise_keys(0, RE)
+        interleave_keys(0, IM)
         quantise_queries(0, 3)
-        project_queries(1, 1)
-        score_rows(0, 0)
+        quantise_keys(0, IM)
         project_keys(1, IM)
         interleave_keys(1, RE)
-        add_query_bias(1, 1, RE)
-        add_query_bias(1, 1, IM)
+        project_queries(1, 0)
         quantise_keys(1, RE)
-        quantise_queries(1, 0)
-        project_queries(1, 2)
+        score_rows(0, 0)
+        add_query_bias(1, 0, RE)
+        add_query_bias(1, 0, IM)
+        project_queries(1, 1)
         score_rows(0, 1)
-        score_rows(0, 2)
-        add_query_bias(1, 2, RE)
         interleave_keys(1, IM)
-        add_query_bias(1, 2, IM)
+        add_query_bias(1, 1, RE)
+        quantise_queries(1, 0)
+        add_query_bias(1, 1, IM)
+        project_queries(1, 2)
+        score_rows(0, 2)
         quantise_keys(1, IM)
         quantise_queries(1, 1)
+        add_query_bias(1, 2, RE)
+        add_query_bias(1, 2, IM)
         project_queries(1, 3)
         score_rows(0, 3)
         add_query_bias(1, 3, RE)

@@ -127,8 +127,8 @@ def tile_teleportationattention_pa_kernel(
         def part_major_column(b, part, j):
             return ((b * 2 + part) * GROUPS + j) * P
 
-        def group_major_column(b, part, j):
-            return ((b * GROUPS + j) * 2 + part) * P
+        def query_column(b, part, j):
+            return ((b * GROUPS + j) * 2 + part) * P if b == 0 else part_major_column(b, part, j)
 
         def split_pairs(piece, copy):
             split = work.tile([P, PIECE], BF16, tag="split", bufs=8, align_bytes=64)
@@ -185,53 +185,75 @@ def tile_teleportationattention_pa_kernel(
         q_banks = {}
         q_values = {}
 
-        def project_queries(b, j):
-            for part in (RE, IM):
-                bank = psum.tile([P, BANK], F32, tag="bank")
-                for t in range(PACK):
-                    project(bank[:, t * P : (t + 1) * P], "q", part, t, b, j)
-                q_banks[b, j, part] = bank
+        q_banks = {}
+        q_values = {}
 
-        def add_query_bias(b, j, part):
-            if part == RE:
-                q_values[b, j] = work.tile([P, 2 * BANK], BF16, tag="grouped_q", name="grouped_q", bufs=8, align_bytes=64)
+        def project_group(b, part, j):
+            bank = psum.tile([P, BANK], F32, tag="bank")
+            for t in range(PACK):
+                project(bank[:, t * P : (t + 1) * P], "q", part, t, b, j)
+            q_banks[b, part, j] = bank
+
+        def add_group_bias(b, part, j, values):
             nc.vector.tensor_tensor(
-                out=q_values[b, j][:, part * BANK : (part + 1) * BANK].rearrange("p (n t) -> p n t", t=PACK),
-                in0=q_banks[b, j, part][:].rearrange("p (t n) -> p n t", t=PACK),
+                out=values.rearrange("p (n t) -> p n t", t=PACK),
+                in0=q_banks[b, part, j][:].rearrange("p (t n) -> p n t", t=PACK),
                 in1=bias["q", part].unsqueeze(1).to_broadcast([P, P, PACK]),
                 op=mybir.AluOpType.add,
             )
 
-        def quantise_queries(b, j):
-            quantise(nc, queries, group_major_column(b, RE, j), q_values[b, j][:])
+        def new_pair_of_values():
+            return work.tile([P, 2 * BANK], BF16, tag="grouped_q", name="grouped_q", bufs=8, align_bytes=64)
 
-        k_planes = {}
-        k_values = {}
+        def project_queries(j):
+            project_group(0, RE, j)
+            project_group(0, IM, j)
 
-        def project_keys(b, part):
-            planes = work.tile([P, PACK * TOKENS], BF16, tag="planes", bufs=2)
+        def add_query_bias(j):
+            q_values[0, j] = new_pair_of_values()
+            for part in (RE, IM):
+                add_group_bias(0, part, j, q_values[0, j][:, part * BANK : (part + 1) * BANK])
+
+        def quantise_queries(j):
+            quantise(nc, queries, query_column(0, RE, j), q_values[0, j][:])
+
+        def add_im_query_bias(j):
+            if j % 2 == 0:
+                q_values[1, j // 2] = new_pair_of_values()
+            half = j % 2
+            add_group_bias(1, IM, j, q_values[1, j // 2][:, half * BANK : (half + 1) * BANK])
+
+        def quantise_im_queries(pair):
+            quantise(nc, queries, query_column(1, IM, 2 * pair), q_values[1, pair][:])
+
+        all_planes = {}
+        all_values = {}
+
+        def project_all(kind, b, part):
+            planes = work.tile([P, PACK * TOKENS], BF16, tag="planes", bufs=3)
             for t in range(PACK):
                 bank = psum.tile([P, BANK], F32, tag="bank")
-                project(bank[:], "k", part, t, b, 0)
+                project(bank[:], kind, part, t, b, 0)
                 nc.scalar.activation(
                     out=planes[:, t * TOKENS : (t + 1) * TOKENS],
                     in_=bank[:],
                     func=mybir.ActivationFunctionType.Identity,
-                    bias=bias["k", part][:, t : t + 1],
+                    bias=bias[kind, part][:, t : t + 1],
                     scale=1.0,
                 )
-            k_planes[b, part] = planes
+            all_planes[kind, b, part] = planes
 
-        def interleave_keys(b, part):
-            grouped = work.tile([P, PACK * TOKENS], BF16, tag="grouped_k", bufs=2, align_bytes=64)
+        def interleave_all(kind, b, part):
+            values = work.tile([P, PACK * TOKENS], BF16, tag="all_values", bufs=3, align_bytes=64)
             nc.vector.tensor_copy(
-                out=grouped[:].rearrange("p (c i t) -> p c t i", i=4, t=PACK),
-                in_=k_planes[b, part][:].rearrange("p (t c i) -> p c t i", i=4, t=PACK),
+                out=values[:].rearrange("p (c i t) -> p c t i", i=4, t=PACK),
+                in_=all_planes[kind, b, part][:].rearrange("p (t c i) -> p c t i", i=4, t=PACK),
             )
-            k_values[b, part] = grouped
+            all_values[kind, b, part] = values
 
-        def quantise_keys(b, part):
-            quantise(nc, keys, part_major_column(b, part, 0), k_values[b, part][:])
+        def quantise_all(kind, b, part):
+            operand = {"k": keys, "q": queries}[kind]
+            quantise(nc, operand, part_major_column(b, part, 0), all_values[kind, b, part][:])
 
         def score_passes(acc, b, j, first_key):
             for part in (RE, IM):
@@ -239,7 +261,7 @@ def tile_teleportationattention_pa_kernel(
                     nc,
                     acc,
                     queries,
-                    group_major_column(b, part, j),
+                    query_column(b, part, j),
                     keys,
                     part_major_column(b, part, 0) + first_key,
                     part == RE,
@@ -289,71 +311,66 @@ def tile_teleportationattention_pa_kernel(
             for part in (IM, RE):
                 raw_w["k", part][c] = split_pairs(raw_w["k", part][c], nc.vector.tensor_copy)
         quantise_tokens(0, 1)
-        project_queries(0, 0)
+        project_queries(0)
         transpose_weight("k", 0)
         transpose_weight("k", 1)
         for half in range(2):
             for part in (RE, IM):
                 raw_x[1, part][half] = split_pairs(raw_x[1, part][half], nc.scalar.copy)
-        project_queries(0, 1)
-        add_query_bias(0, 0, RE)
-        add_query_bias(0, 0, IM)
+        project_queries(1)
+        add_query_bias(0)
         for c in range(2):
             negate_weight("k", c)
             quantise_weight("k", "re", c)
             quantise_weight("k", "im_neg", c)
             if c == 0:
-                project_queries(0, 2)
-                add_query_bias(0, 1, RE)
-                add_query_bias(0, 1, IM)
-        project_keys(0, RE)
+                project_queries(2)
+                add_query_bias(1)
+
+        project_all("k", 0, RE)
         quantise_weight("k", "im", 0)
         quantise_weight("k", "im", 1)
-        add_query_bias(0, 2, RE)
-        add_query_bias(0, 2, IM)
-        quantise_queries(0, 0)
-        quantise_queries(0, 1)
-        quantise_queries(0, 2)
+        add_query_bias(2)
+        for j in range(3):
+            quantise_queries(j)
         transpose_tokens(1, 0)
         transpose_tokens(1, 1)
-        project_keys(0, IM)
+        project_all("k", 0, IM)
         quantise_tokens(1, 0)
-        project_queries(0, 3)
-        interleave_keys(0, RE)
+        project_queries(3)
+        interleave_all("k", 0, RE)
         quantise_tokens(1, 1)
-        add_query_bias(0, 3, RE)
-        add_query_bias(0, 3, IM)
-        project_keys(1, RE)
-        quantise_keys(0, RE)
-        interleave_keys(0, IM)
-        quantise_queries(0, 3)
-        quantise_keys(0, IM)
-        project_keys(1, IM)
-        interleave_keys(1, RE)
-        project_queries(1, 0)
-        quantise_keys(1, RE)
+        add_query_bias(3)
+
+        project_all("k", 1, RE)
+        quantise_all("k", 0, RE)
+        interleave_all("k", 0, IM)
+        quantise_queries(3)
+        quantise_all("k", 0, IM)
+        project_group(1, IM, 0)
+        project_all("k", 1, IM)
+        add_im_query_bias(0)
+        interleave_all("k", 1, RE)
+        project_group(1, IM, 1)
+        project_all("q", 1, RE)
+        add_im_query_bias(1)
+        quantise_all("k", 1, RE)
+        interleave_all("k", 1, IM)
+        quantise_im_queries(0)
         score_rows(0, 0)
-        add_query_bias(1, 0, RE)
-        add_query_bias(1, 0, IM)
-        project_queries(1, 1)
+        quantise_all("k", 1, IM)
+        project_group(1, IM, 2)
         score_rows(0, 1)
-        interleave_keys(1, IM)
-        add_query_bias(1, 1, RE)
-        quantise_queries(1, 0)
-        add_query_bias(1, 1, IM)
-        project_queries(1, 2)
+        interleave_all("q", 1, RE)
+        add_im_query_bias(2)
+        quantise_all("q", 1, RE)
+        project_group(1, IM, 3)
         score_rows(0, 2)
-        quantise_keys(1, IM)
-        quantise_queries(1, 1)
-        add_query_bias(1, 2, RE)
-        add_query_bias(1, 2, IM)
-        project_queries(1, 3)
         score_rows(0, 3)
-        add_query_bias(1, 3, RE)
-        quantise_queries(1, 2)
-        add_query_bias(1, 3, IM)
+        add_im_query_bias(3)
+
         score_rows(1, 0)
         score_rows(1, 1)
-        quantise_queries(1, 3)
+        quantise_im_queries(1)
         score_rows(1, 2)
         last_score_rows(1, 3)

@@ -25,8 +25,8 @@ FLOPS = 8 * 2 * BATCH * TOKENS * FEATURES * FEATURES + 2 * 2 * BATCH * TOKENS * 
 
 
 def new_mx_operand(pool, name, columns):
-    codes = pool.tile([P, columns], U32, name=name + "_codes", align_bytes=64)
-    scales = pool.tile([P, columns], U8, name=name + "_scales", align_bytes=64)
+    codes = pool.tile([P, columns], U32, name=name + "_codes", align_bytes=256)
+    scales = pool.tile([P, columns], U8, name=name + "_scales", align_bytes=256)
     return {"codes": codes, "scales": scales}
 
 
@@ -181,9 +181,6 @@ def tile_teleportationattention_pa_kernel(
             w_of_x_re, w_of_x_im = (("re", "im_neg"), ("im", "re"))[part]
             mx_pass(nc, acc, weight[kind, w_of_x_re], t * P, tokens, part_major_column(b, RE, j), True, False)
             mx_pass(nc, acc, weight[kind, w_of_x_im], t * P, tokens, part_major_column(b, IM, j), False, True)
-
-        q_banks = {}
-        q_values = {}
 
         q_banks = {}
         q_values = {}

@@ -87,20 +87,20 @@ def tile_teleportationattention_pa_kernel(
         raw_w = {}
         raw_x = {}
 
-        def load_weights(kind, w_re, w_im):
-            raw_w[kind, RE] = []
-            raw_w[kind, IM] = []
-            for c in range(2):
+        def load_weights(kind, w_re, w_im, cs=(0, 1)):
+            raw_w.setdefault((kind, RE), [])
+            raw_w.setdefault((kind, IM), [])
+            for c in cs:
                 for part, name, matrix in ((IM, "im", w_im), (RE, "re", w_re)):
                     rows = matrix.rearrange("(r j) d -> r (j d)", j=GROUPS)
                     raw_w[kind, part].append(
                         load("raw_w" + kind + "_" + name + str(c), rows[:, c * PIECE : (c + 1) * PIECE])
                     )
 
-        def load_tokens(b):
-            raw_x[b, RE] = []
-            raw_x[b, IM] = []
-            for half in range(2):
+        def load_tokens(b, halves=(0, 1)):
+            raw_x.setdefault((b, RE), [])
+            raw_x.setdefault((b, IM), [])
+            for half in halves:
                 tail = str(b) + "_" + str(half)
                 for part, name, matrix in ((RE, "re", x_re), (IM, "im", x_im)):
                     rows = matrix[b, half * 256 : (half + 1) * 256, :].rearrange("(r i) d -> r (i d)", i=2)
@@ -138,7 +138,7 @@ def tile_teleportationattention_pa_kernel(
             )
             return split[:]
 
-        def features_to_partitions(piece, is_split=False):
+        def features_to_partitions(piece, is_split=False, copy=None):
             raw_pairs = piece.bitcast(F32)
             grouped = work.tile([P, PIECE], BF16, tag="grouped_in", bufs=8, align_bytes=64)
             bank = psum.tile([P, BANK], F32, tag="bank")
@@ -147,18 +147,26 @@ def tile_teleportationattention_pa_kernel(
                 first = (s // 2) * 2 * P + s % 2
                 words = columns if is_split else slice(first, first + 2 * P - 1, 2)
                 nc.tensor.transpose(bank[:, columns], raw_pairs[:, words], ident[:])
-            nc.scalar.copy(
+            (copy or nc.scalar.copy)(
                 out=grouped[:].bitcast(F32).rearrange("p (j r u) -> p j r u", j=2, u=2),
                 in_=bank[:].rearrange("p (j u r) -> p j r u", j=2, u=2),
             )
             return grouped
 
         w_grouped = {}
+        is_split = set()
         x_grouped = {}
 
-        def transpose_weight(kind, c):
-            for part in (IM, RE):
-                w_grouped[kind, part, c] = features_to_partitions(raw_w[kind, part][c], kind == "k")
+        def split_weight(kind, c, part, copy):
+            raw_w[kind, part][c] = split_pairs(raw_w[kind, part][c], copy)
+            is_split.add(("w", kind, part, c))
+
+        def split_tokens(b, half, part, copy):
+            raw_x[b, part][half] = split_pairs(raw_x[b, part][half], copy)
+            is_split.add(("x", b, part, half))
+
+        def transpose_weight(kind, c, part, copy=None):
+            w_grouped[kind, part, c] = features_to_partitions(raw_w[kind, part][c], ("w", kind, part, c) in is_split, copy)
 
         def negate_weight(kind, c):
             negated = work.tile([P, PIECE], BF16, tag="negated", align_bytes=64)
@@ -169,13 +177,11 @@ def tile_teleportationattention_pa_kernel(
             source = {"re": RE, "im": IM, "im_neg": "neg"}[name]
             quantise(nc, weight[kind, name], c * PIECE // PACK, w_grouped[kind, source, c][:])
 
-        def transpose_tokens(b, half):
-            for part in (RE, IM):
-                x_grouped[b, part, half] = features_to_partitions(raw_x[b, part][half], b == 1)
+        def transpose_tokens(b, half, part, copy=None):
+            x_grouped[b, part, half] = features_to_partitions(raw_x[b, part][half], ("x", b, part, half) in is_split, copy)
 
-        def quantise_tokens(b, half):
-            for part in (RE, IM):
-                quantise(nc, tokens, part_major_column(b, part, 2 * half), x_grouped[b, part, half][:])
+        def quantise_tokens(b, half, part):
+            quantise(nc, tokens, part_major_column(b, part, 2 * half), x_grouped[b, part, half][:])
 
         def project(acc, kind, part, t, b, j):
             w_of_x_re, w_of_x_im = (("re", "im_neg"), ("im", "re"))[part]
@@ -185,11 +191,12 @@ def tile_teleportationattention_pa_kernel(
         q_banks = {}
         q_values = {}
 
-        def project_group(b, part, j):
-            bank = psum.tile([P, BANK], F32, tag="bank")
-            for t in range(PACK):
-                project(bank[:, t * P : (t + 1) * P], "q", part, t, b, j)
-            q_banks[b, part, j] = bank
+        def project_group(b, part, j, ts=(0, 1, 2, 3)):
+            if ts[0] == 0:
+                bank = psum.tile([P, BANK], F32, tag="bank")
+                q_banks[b, part, j] = bank
+            for t in ts:
+                project(q_banks[b, part, j][:, t * P : (t + 1) * P], "q", part, t, b, j)
 
         def add_group_bias(b, part, j, values):
             nc.vector.tensor_tensor(
@@ -226,18 +233,38 @@ def tile_teleportationattention_pa_kernel(
         all_planes = {}
         all_values = {}
 
+        HALF = TOKENS // 2
+        quarter_banks = {}
+
+        def project_quarter(b, part, pair, half):
+            bank = psum.tile([P, BANK], F32, tag="bank")
+            for i in range(2):
+                project(bank[:, i * HALF : (i + 1) * HALF], "q", part, 2 * pair + i, b, 2 * half)
+            quarter_banks[b, part, pair, half] = bank
+
+        def add_quarter_bias(b, part, pair, half):
+            if ("q", b, part) not in all_planes:
+                all_planes["q", b, part] = work.tile([P, PACK * TOKENS], BF16, tag="planes", name="planes", bufs=3)
+            for i in range(2):
+                t = 2 * pair + i
+                first = t * TOKENS + half * HALF
+                add_bias(
+                    all_planes["q", b, part][:, first : first + HALF],
+                    quarter_banks[b, part, pair, half][:, i * HALF : (i + 1) * HALF],
+                    bias["q", part][:, t : t + 1],
+                )
+
+        def add_bias(out, acc, column):
+            nc.scalar.activation(out=out, in_=acc, func=mybir.ActivationFunctionType.Identity, bias=column, scale=1.0)
+
+        all_banks = {}
+
         def project_all(kind, b, part):
             planes = work.tile([P, PACK * TOKENS], BF16, tag="planes", bufs=3)
             for t in range(PACK):
                 bank = psum.tile([P, BANK], F32, tag="bank")
                 project(bank[:], kind, part, t, b, 0)
-                nc.scalar.activation(
-                    out=planes[:, t * TOKENS : (t + 1) * TOKENS],
-                    in_=bank[:],
-                    func=mybir.ActivationFunctionType.Identity,
-                    bias=bias[kind, part][:, t : t + 1],
-                    scale=1.0,
-                )
+                add_bias(planes[:, t * TOKENS : (t + 1) * TOKENS], bank[:], bias[kind, part][:, t : t + 1])
             all_planes[kind, b, part] = planes
 
         def interleave_all(kind, b, part):
@@ -247,6 +274,27 @@ def tile_teleportationattention_pa_kernel(
                 in_=all_planes[kind, b, part][:].rearrange("p (t c i) -> p c t i", i=4, t=PACK),
             )
             all_values[kind, b, part] = values
+
+        def interleave_half(kind, b, part, half):
+            if half == 0:
+                all_values[kind, b, part] = work.tile(
+                    [P, PACK * TOKENS], BF16, tag="all_values", name="all_values", bufs=3, align_bytes=64
+                )
+            planes = all_planes[kind, b, part][:].rearrange("p (t n) -> p t n", t=PACK)[:, :, half * HALF : (half + 1) * HALF]
+            values = all_values[kind, b, part][:, half * PACK * HALF : (half + 1) * PACK * HALF]
+            nc.vector.tensor_copy(
+                out=values.rearrange("p (c i t) -> p c t i", i=4, t=PACK),
+                in_=planes.rearrange("p t (c i) -> p c t i", i=4),
+            )
+
+        def quantise_half(kind, b, part, half):
+            operand = {"k": keys, "q": queries}[kind]
+            quantise(
+                nc,
+                operand,
+                part_major_column(b, part, 2 * half),
+                all_values[kind, b, part][:, half * PACK * HALF : (half + 1) * PACK * HALF],
+            )
 
         def quantise_all(kind, b, part):
             operand = {"k": keys, "q": queries}[kind]
@@ -289,31 +337,38 @@ def tile_teleportationattention_pa_kernel(
                 )
                 queue.dma_start(out=rows_of_group(b, j)[:, half * 2 * P : (half + 1) * 2 * P], in_=rows[:])
 
+        V = nc.vector.tensor_copy
+        A = nc.scalar.copy
         for c in range(2):
-            transpose_weight("q", c)
+            for part in (IM, RE):
+                transpose_weight("q", c, part)
             keep_warm(1)
-        transpose_tokens(0, 0)
+        for part in (RE, IM):
+            transpose_tokens(0, 0, part)
         keep_warm(1)
-        transpose_tokens(0, 1)
+        for part in (RE, IM):
+            transpose_tokens(0, 1, part)
         for c in range(2):
             negate_weight("q", c)
             if c == 0:
                 quantise_weight("q", "im", c)
             quantise_weight("q", "re", c)
             quantise_weight("q", "im_neg", c)
-        quantise_tokens(0, 0)
+        for part in (RE, IM):
+            quantise_tokens(0, 0, part)
         quantise_weight("q", "im", 1)
-
         for c in range(2):
             for part in (IM, RE):
-                raw_w["k", part][c] = split_pairs(raw_w["k", part][c], nc.vector.tensor_copy)
-        quantise_tokens(0, 1)
+                split_weight("k", c, part, V)
+        for part in (RE, IM):
+            quantise_tokens(0, 1, part)
         project_queries(0)
-        transpose_weight("k", 0)
-        transpose_weight("k", 1)
+        for c in range(2):
+            for part in (IM, RE):
+                transpose_weight("k", c, part)
         for half in range(2):
             for part in (RE, IM):
-                raw_x[1, part][half] = split_pairs(raw_x[1, part][half], nc.scalar.copy)
+                split_tokens(1, half, part, A)
         project_queries(1)
         add_query_bias(0)
         for c in range(2):
@@ -322,23 +377,24 @@ def tile_teleportationattention_pa_kernel(
             quantise_weight("k", "im_neg", c)
             if c == 0:
                 project_queries(2)
-                add_query_bias(1)
-
+        add_query_bias(1)
         project_all("k", 0, RE)
+        add_query_bias(2)
         quantise_weight("k", "im", 0)
         quantise_weight("k", "im", 1)
-        add_query_bias(2)
         for j in range(3):
             quantise_queries(j)
-        transpose_tokens(1, 0)
-        transpose_tokens(1, 1)
+        for half in range(2):
+            for part in (RE, IM):
+                transpose_tokens(1, half, part)
         project_all("k", 0, IM)
-        quantise_tokens(1, 0)
+        for part in (RE, IM):
+            quantise_tokens(1, 0, part)
         project_queries(3)
         interleave_all("k", 0, RE)
-        quantise_tokens(1, 1)
+        for part in (RE, IM):
+            quantise_tokens(1, 1, part)
         add_query_bias(3)
-
         project_all("k", 1, RE)
         quantise_all("k", 0, RE)
         interleave_all("k", 0, IM)
@@ -349,23 +405,30 @@ def tile_teleportationattention_pa_kernel(
         add_im_query_bias(0)
         interleave_all("k", 1, RE)
         project_group(1, IM, 1)
-        project_all("q", 1, RE)
+        project_group(1, IM, 2)
         add_im_query_bias(1)
         quantise_all("k", 1, RE)
+        for half in range(2):
+            for pair in range(2):
+                project_quarter(1, RE, pair, half)
+        for pair in range(2):
+            add_quarter_bias(1, RE, pair, 0)
         interleave_all("k", 1, IM)
         quantise_im_queries(0)
-        score_rows(0, 0)
-        quantise_all("k", 1, IM)
-        project_group(1, IM, 2)
-        score_rows(0, 1)
-        interleave_all("q", 1, RE)
         add_im_query_bias(2)
-        quantise_all("q", 1, RE)
+        for pair in range(2):
+            add_quarter_bias(1, RE, pair, 1)
+        quantise_all("k", 1, IM)
+        interleave_half("q", 1, RE, 0)
+        score_rows(0, 0)
         project_group(1, IM, 3)
+        score_rows(0, 1)
         score_rows(0, 2)
         score_rows(0, 3)
+        interleave_half("q", 1, RE, 1)
+        quantise_half("q", 1, RE, 0)
         add_im_query_bias(3)
-
+        quantise_half("q", 1, RE, 1)
         score_rows(1, 0)
         score_rows(1, 1)
         quantise_im_queries(1)

@@ -242,14 +242,16 @@ def tile_teleportationattention_pa_kernel(
                 project(bank[:, i * HALF : (i + 1) * HALF], "q", part, 2 * pair + i, b, 2 * half)
             quarter_banks[b, part, pair, half] = bank
 
+        half_planes = {}
+        half_values = {}
+
         def add_quarter_bias(b, part, pair, half):
-            if ("q", b, part) not in all_planes:
-                all_planes["q", b, part] = work.tile([P, PACK * TOKENS], BF16, tag="planes", name="planes", bufs=3)
+            if pair == 0:
+                half_planes[b, part, half] = work.tile([P, PACK * HALF], BF16, tag="half_planes", name="half_planes", bufs=4)
             for i in range(2):
                 t = 2 * pair + i
-                first = t * TOKENS + half * HALF
                 add_bias(
-                    all_planes["q", b, part][:, first : first + HALF],
+                    half_planes[b, part, half][:, t * HALF : (t + 1) * HALF],
                     quarter_banks[b, part, pair, half][:, i * HALF : (i + 1) * HALF],
                     bias["q", part][:, t : t + 1],
                 )
@@ -275,26 +277,16 @@ def tile_teleportationattention_pa_kernel(
             )
             all_values[kind, b, part] = values
 
-        def interleave_half(kind, b, part, half):
-            if half == 0:
-                all_values[kind, b, part] = work.tile(
-                    [P, PACK * TOKENS], BF16, tag="all_values", name="all_values", bufs=3, align_bytes=64
-                )
-            planes = all_planes[kind, b, part][:].rearrange("p (t n) -> p t n", t=PACK)[:, :, half * HALF : (half + 1) * HALF]
-            values = all_values[kind, b, part][:, half * PACK * HALF : (half + 1) * PACK * HALF]
+        def interleave_half(b, part, half):
+            values = work.tile([P, PACK * HALF], BF16, tag="half_values", bufs=4, align_bytes=64)
             nc.vector.tensor_copy(
-                out=values.rearrange("p (c i t) -> p c t i", i=4, t=PACK),
-                in_=planes.rearrange("p t (c i) -> p c t i", i=4),
+                out=values[:].rearrange("p (c i t) -> p c t i", i=4, t=PACK),
+                in_=half_planes[b, part, half][:].rearrange("p (t c i) -> p c t i", i=4, t=PACK),
             )
+            half_values[b, part, half] = values
 
-        def quantise_half(kind, b, part, half):
-            operand = {"k": keys, "q": queries}[kind]
-            quantise(
-                nc,
-                operand,
-                part_major_column(b, part, 2 * half),
-                all_values[kind, b, part][:, half * PACK * HALF : (half + 1) * PACK * HALF],
-            )
+        def quantise_half(b, part, half):
+            quantise(nc, queries, query_column(b, part, 2 * half), half_values[b, part, half][:])
 
         def quantise_all(kind, b, part):
             operand = {"k": keys, "q": queries}[kind]
@@ -405,32 +397,33 @@ def tile_teleportationattention_pa_kernel(
         add_im_query_bias(0)
         interleave_all("k", 1, RE)
         project_group(1, IM, 1)
-        project_group(1, IM, 2)
+        score_rows(0, 0)
         add_im_query_bias(1)
         quantise_all("k", 1, RE)
-        for half in range(2):
-            for pair in range(2):
-                project_quarter(1, RE, pair, half)
+        for pair in range(2):
+            project_quarter(1, RE, pair, 0)
+        for pair in range(2):
+            project_quarter(1, RE, pair, 1)
         for pair in range(2):
             add_quarter_bias(1, RE, pair, 0)
         interleave_all("k", 1, IM)
-        quantise_im_queries(0)
-        add_im_query_bias(2)
         for pair in range(2):
             add_quarter_bias(1, RE, pair, 1)
-        quantise_all("k", 1, IM)
-        interleave_half("q", 1, RE, 0)
-        score_rows(0, 0)
-        project_group(1, IM, 3)
         score_rows(0, 1)
+        quantise_im_queries(0)
+        quantise_all("k", 1, IM)
+        interleave_half(1, RE, 0)
+        project_group(1, IM, 2)
         score_rows(0, 2)
+        interleave_half(1, RE, 1)
+        quantise_half(1, RE, 0)
+        add_im_query_bias(2)
+        project_group(1, IM, 3)
+        quantise_half(1, RE, 1)
         score_rows(0, 3)
-        interleave_half("q", 1, RE, 1)
-        quantise_half("q", 1, RE, 0)
         add_im_query_bias(3)
-        quantise_half("q", 1, RE, 1)
+        quantise_im_queries(1)
         score_rows(1, 0)
         score_rows(1, 1)
-        quantise_im_queries(1)
         score_rows(1, 2)
         last_score_rows(1, 3)

@@ -24,10 +24,10 @@ IM = 1
 FLOPS = 8 * 2 * BATCH * TOKENS * FEATURES * FEATURES + 2 * 2 * BATCH * TOKENS * TOKENS * FEATURES
 
 
-def new_mx_operand(pool, name, columns):
-    codes = pool.tile([P, columns], U32, name=name + "_codes", align_bytes=256)
-    scales = pool.tile([P, columns], U8, name=name + "_scales", align_bytes=256)
-    return {"codes": codes, "scales": scales}
+def new_mx_operand(pool, name, columns, code_shift, scale_shift):
+    codes = pool.tile([P, columns + code_shift // 4], U32, name=name + "_codes", align_bytes=256)
+    scales = pool.tile([P, columns + scale_shift], U8, name=name + "_scales", align_bytes=256)
+    return {"codes": codes[:, code_shift // 4 :], "scales": scales[:, scale_shift:]}
 
 
 def quantise(nc, operand, first, values):
@@ -119,10 +119,10 @@ def tile_teleportationattention_pa_kernel(
         weight = {}
         for kind in ("k", "q"):
             for name in ("re", "im", "im_neg"):
-                weight[kind, name] = new_mx_operand(keep, "w" + kind + "_" + name, FEATURES)
-        tokens = new_mx_operand(keep, "x", BATCH * 2 * TOKENS)
-        keys = new_mx_operand(keep, "k", BATCH * 2 * TOKENS)
-        queries = new_mx_operand(keep, "q", BATCH * 2 * TOKENS)
+                weight[kind, name] = new_mx_operand(keep, "w" + kind + "_" + name, FEATURES, 0, 64)
+        tokens = new_mx_operand(keep, "x", BATCH * 2 * TOKENS, 128, 0)
+        keys = new_mx_operand(keep, "k", BATCH * 2 * TOKENS, 128, 0)
+        queries = new_mx_operand(keep, "q", BATCH * 2 * TOKENS, 0, 64)
 
         def part_major_column(b, part, j):
             return ((b * 2 + part) * GROUPS + j) * P

from contextlib import ExitStack

import concourse.mybir as mybir
from concourse.masks import make_identity

F32 = mybir.dt.float32
BF16 = mybir.dt.bfloat16
U32 = mybir.dt.uint32
U8 = mybir.dt.uint8
FP8X4 = mybir.dt.float8_e4m3fn_x4

P = 128
PACK = 4
BANK = 512
BATCH = 2
TOKENS = 512
FEATURES = 512
GROUPS = 4
PIECE = 2 * FEATURES
WARM_UP = 4
RE = 0
IM = 1

FLOPS = 8 * 2 * BATCH * TOKENS * FEATURES * FEATURES + 2 * 2 * BATCH * TOKENS * TOKENS * FEATURES


def new_mx_operand(pool, name, columns, code_shift, scale_shift):
    codes = pool.tile([P, columns + code_shift // 4], U32, name=name + "_codes", align_bytes=256)
    scales = pool.tile([P, columns + scale_shift], U8, name=name + "_scales", align_bytes=256)
    return {"codes": codes[:, code_shift // 4 :], "scales": scales[:, scale_shift:]}


def quantise(nc, operand, first, values):
    columns = slice(first, first + values.shape[1] // PACK)
    nc.vector.quantize_mx(
        out=operand["codes"][:, columns].bitcast(FP8X4),
        scales=operand["scales"][:, columns],
        in_=values,
    )


def mx_pass(nc, acc, stationary, s_first, moving, m_first, start, stop):
    s_columns = slice(s_first, s_first + P)
    m_columns = slice(m_first, m_first + acc.shape[1])
    nc.tensor.matmul_mx(
        out=acc,
        lhsT=stationary["codes"][:, s_columns].bitcast(FP8X4),
        lhsT_scale=stationary["scales"][:, s_columns],
        rhs=moving["codes"][:, m_columns].bitcast(FP8X4),
        rhs_scale=moving["scales"][:, m_columns],
        start=start,
        stop=stop,
    )


def tile_teleportationattention_pa_kernel(
    tc, x_re, x_im, Wq_re, Wq_im, bq_re, bq_im, Wk_re, Wk_im, bk_re, bk_im, out
):
    nc = tc.nc
    with ExitStack() as ctx:
        keep = ctx.enter_context(tc.tile_pool(name="keep", bufs=1))
        work = ctx.enter_context(tc.tile_pool(name="work", bufs=4))
        psum = ctx.enter_context(tc.psum_pool(name="psum", bufs=8))
        ctx.enter_context(tc.manual_schedule())

        ident = keep.tile([P, P], F32, name="ident")
        make_identity(nc, ident[:])

        zeros = keep.tile([P, BANK], BF16, name="zeros")
        nc.vector.memset(zeros[:], 0.0)
        warm = psum.tile([P, BANK], F32, tag="bank")

        def keep_warm(count):
            for n in range(count):
                nc.tensor.matmul(warm[:], lhsT=zeros[:, 0:P], rhs=zeros[:], start=True, stop=True)

        keep_warm(WARM_UP)

        bias_slots = keep.tile([P, 4, 16], BF16, name="bias_slots")
        bias = {}

        def load(name, rows):
            raw = keep.tile([P, PIECE], BF16, name=name)
            nc.sync.dma_start(out=raw[:], in_=rows)
            return raw[:]

        raw_w = {}
        raw_x = {}

        def load_weights(kind, w_re, w_im, cs=(0, 1)):
            raw_w.setdefault((kind, RE), [])
            raw_w.setdefault((kind, IM), [])
            for c in cs:
                for part, name, matrix in ((IM, "im", w_im), (RE, "re", w_re)):
                    rows = matrix.rearrange("(r j) d -> r (j d)", j=GROUPS)
                    raw_w[kind, part].append(
                        load("raw_w" + kind + "_" + name + str(c), rows[:, c * PIECE : (c + 1) * PIECE])
                    )

        def load_tokens(b, halves=(0, 1)):
            raw_x.setdefault((b, RE), [])
            raw_x.setdefault((b, IM), [])
            for half in halves:
                tail = str(b) + "_" + str(half)
                for part, name, matrix in ((RE, "re", x_re), (IM, "im", x_im)):
                    rows = matrix[b, half * 256 : (half + 1) * 256, :].rearrange("(r i) d -> r (i d)", i=2)
                    raw_x[b, part].append(load("raw_x_" + name + tail, rows))

        load_weights("q", Wq_re, Wq_im)
        load_tokens(0)
        for n, (kind, part, vector) in enumerate(
            (("q", RE, bq_re), ("q", IM, bq_im), ("k", RE, bk_re), ("k", IM, bk_im))
        ):
            bias[kind, part] = bias_slots[:, n, 0:PACK]
            nc.sync.dma_start(out=bias[kind, part], in_=vector.rearrange("(r t) -> r t", t=PACK))
        load_weights("k", Wk_re, Wk_im)
        load_tokens(1)

        weight = {}
        for kind in ("k", "q"):
            for name in ("re", "im", "im_neg"):
                weight[kind, name] = new_mx_operand(keep, "w" + kind + "_" + name, FEATURES, 0, 64)
        tokens = new_mx_operand(keep, "x", BATCH * 2 * TOKENS, 128, 0)
        keys = new_mx_operand(keep, "k", BATCH * 2 * TOKENS, 128, 0)
        queries = new_mx_operand(keep, "q", BATCH * 2 * TOKENS, 0, 64)

        def part_major_column(b, part, j):
            return ((b * 2 + part) * GROUPS + j) * P

        def query_column(b, part, j):
            return ((b * GROUPS + j) * 2 + part) * P if b == 0 else part_major_column(b, part, j)

        def split_pairs(piece, copy):
            split = work.tile([P, PIECE], BF16, tag="split", bufs=8, align_bytes=64)
            copy(
                out=split[:].bitcast(F32).rearrange("q (j u p) -> q j u p", j=2, u=2),
                in_=piece.bitcast(F32).rearrange("q (j p u) -> q j u p", j=2, u=2),
            )
            return split[:]

        def features_to_partitions(piece, is_split=False, copy=None):
            raw_pairs = piece.bitcast(F32)
            grouped = work.tile([P, PIECE], BF16, tag="grouped_in", bufs=8, align_bytes=64)
            bank = psum.tile([P, BANK], F32, tag="bank")
            for s in range(4):
                columns = slice(s * P, (s + 1) * P)
                first = (s // 2) * 2 * P + s % 2
                words = columns if is_split else slice(first, first + 2 * P - 1, 2)
                nc.tensor.transpose(bank[:, columns], raw_pairs[:, words], ident[:])
            (copy or nc.scalar.copy)(
                out=grouped[:].bitcast(F32).rearrange("p (j r u) -> p j r u", j=2, u=2),
                in_=bank[:].rearrange("p (j u r) -> p j r u", j=2, u=2),
            )
            return grouped

        w_grouped = {}
        is_split = set()
        x_grouped = {}

        def split_weight(kind, c, part, copy):
            raw_w[kind, part][c] = split_pairs(raw_w[kind, part][c], copy)
            is_split.add(("w", kind, part, c))

        def split_tokens(b, half, part, copy):
            raw_x[b, part][half] = split_pairs(raw_x[b, part][half], copy)
            is_split.add(("x", b, part, half))

        def transpose_weight(kind, c, part, copy=None):
            w_grouped[kind, part, c] = features_to_partitions(raw_w[kind, part][c], ("w", kind, part, c) in is_split, copy)

        def negate_weight(kind, c):
            negated = work.tile([P, PIECE], BF16, tag="negated", align_bytes=64)
            nc.vector.tensor_scalar_mul(out=negated[:], in0=w_grouped[kind, IM, c][:], scalar1=-1.0)
            w_grouped[kind, "neg", c] = negated

        def quantise_weight(kind, name, c):
            source = {"re": RE, "im": IM, "im_neg": "neg"}[name]
            quantise(nc, weight[kind, name], c * PIECE // PACK, w_grouped[kind, source, c][:])

        def transpose_tokens(b, half, part, copy=None):
            x_grouped[b, part, half] = features_to_partitions(raw_x[b, part][half], ("x", b, part, half) in is_split, copy)

        def quantise_tokens(b, half, part):
            quantise(nc, tokens, part_major_column(b, part, 2 * half), x_grouped[b, part, half][:])

        def project(acc, kind, part, t, b, j):
            w_of_x_re, w_of_x_im = (("re", "im_neg"), ("im", "re"))[part]
            mx_pass(nc, acc, weight[kind, w_of_x_re], t * P, tokens, part_major_column(b, RE, j), True, False)
            mx_pass(nc, acc, weight[kind, w_of_x_im], t * P, tokens, part_major_column(b, IM, j), False, True)

        q_banks = {}
        q_values = {}

        def project_group(b, part, j, ts=(0, 1, 2, 3)):
            if ts[0] == 0:
                bank = psum.tile([P, BANK], F32, tag="bank")
                q_banks[b, part, j] = bank
            for t in ts:
                project(q_banks[b, part, j][:, t * P : (t + 1) * P], "q", part, t, b, j)

        def add_group_bias(b, part, j, values):
            nc.vector.tensor_tensor(
                out=values.rearrange("p (n t) -> p n t", t=PACK),
                in0=q_banks[b, part, j][:].rearrange("p (t n) -> p n t", t=PACK),
                in1=bias["q", part].unsqueeze(1).to_broadcast([P, P, PACK]),
                op=mybir.AluOpType.add,
            )

        def new_pair_of_values():
            return work.tile([P, 2 * BANK], BF16, tag="grouped_q", name="grouped_q", bufs=8, align_bytes=64)

        def project_queries(j):
            project_group(0, RE, j)
            project_group(0, IM, j)

        def add_query_bias(j):
            q_values[0, j] = new_pair_of_values()
            for part in (RE, IM):
                add_group_bias(0, part, j, q_values[0, j][:, part * BANK : (part + 1) * BANK])

        def quantise_queries(j):
            quantise(nc, queries, query_column(0, RE, j), q_values[0, j][:])

        def add_im_query_bias(j):
            if j % 2 == 0:
                q_values[1, j // 2] = new_pair_of_values()
            half = j % 2
            add_group_bias(1, IM, j, q_values[1, j // 2][:, half * BANK : (half + 1) * BANK])

        def quantise_im_queries(pair):
            quantise(nc, queries, query_column(1, IM, 2 * pair), q_values[1, pair][:])

        all_planes = {}
        all_values = {}

        HALF = TOKENS // 2
        quarter_banks = {}

        def project_quarter(b, part, pair, half):
            bank = psum.tile([P, BANK], F32, tag="bank")
            for i in range(2):
                project(bank[:, i * HALF : (i + 1) * HALF], "q", part, 2 * pair + i, b, 2 * half)
            quarter_banks[b, part, pair, half] = bank

        half_planes = {}
        half_values = {}

        def add_quarter_bias(b, part, pair, half):
            if pair == 0:
                half_planes[b, part, half] = work.tile([P, PACK * HALF], BF16, tag="half_planes", name="half_planes", bufs=4)
            for i in range(2):
                t = 2 * pair + i
                add_bias(
                    half_planes[b, part, half][:, t * HALF : (t + 1) * HALF],
                    quarter_banks[b, part, pair, half][:, i * HALF : (i + 1) * HALF],
                    bias["q", part][:, t : t + 1],
                )

        def add_bias(out, acc, column):
            nc.scalar.activation(out=out, in_=acc, func=mybir.ActivationFunctionType.Identity, bias=column, scale=1.0)

        all_banks = {}

        def project_all(kind, b, part):
            planes = work.tile([P, PACK * TOKENS], BF16, tag="planes", bufs=3)
            for t in range(PACK):
                bank = psum.tile([P, BANK], F32, tag="bank")
                project(bank[:], kind, part, t, b, 0)
                add_bias(planes[:, t * TOKENS : (t + 1) * TOKENS], bank[:], bias[kind, part][:, t : t + 1])
            all_planes[kind, b, part] = planes

        def interleave_all(kind, b, part):
            values = work.tile([P, PACK * TOKENS], BF16, tag="all_values", bufs=3, align_bytes=64)
            nc.vector.tensor_copy(
                out=values[:].rearrange("p (c i t) -> p c t i", i=4, t=PACK),
                in_=all_planes[kind, b, part][:].rearrange("p (t c i) -> p c t i", i=4, t=PACK),
            )
            all_values[kind, b, part] = values

        def interleave_half(b, part, half):
            values = work.tile([P, PACK * HALF], BF16, tag="half_values", bufs=4, align_bytes=64)
            nc.vector.tensor_copy(
                out=values[:].rearrange("p (c i t) -> p c t i", i=4, t=PACK),
                in_=half_planes[b, part, half][:].rearrange("p (t c i) -> p c t i", i=4, t=PACK),
            )
            half_values[b, part, half] = values

        def quantise_half(b, part, half):
            quantise(nc, queries, query_column(b, part, 2 * half), half_values[b, part, half][:])

        def quantise_all(kind, b, part):
            operand = {"k": keys, "q": queries}[kind]
            quantise(nc, operand, part_major_column(b, part, 0), all_values[kind, b, part][:])

        def score_passes(acc, b, j, first_key):
            for part in (RE, IM):
                mx_pass(
                    nc,
                    acc,
                    queries,
                    query_column(b, part, j),
                    keys,
                    part_major_column(b, part, 0) + first_key,
                    part == RE,
                    part == IM,
                )

        def rows_of_group(b, j):
            return out[b, :, :].rearrange("(h r i) k -> h r i k", h=2, i=2)[j // 2, :, j % 2, :]

        def score_rows(b, j):
            acc = psum.tile([P, BANK], F32, tag="bank")
            score_passes(acc[:], b, j, 0)
            rows = work.tile([P, TOKENS], F32, tag="rows", bufs=8)
            nc.scalar.copy(
                out=rows[:].rearrange("p (h r i) -> p h r i", h=2, i=2),
                in_=acc[:].rearrange("p (h i r) -> p h r i", h=2, i=2),
            )
            nc.sync.dma_start(out=rows_of_group(b, j), in_=rows[:])

        def last_score_rows(b, j):
            for half, copy, queue in ((0, nc.scalar.copy, nc.scalar), (1, nc.vector.tensor_copy, nc.sync)):
                acc = psum.tile([P, BANK], F32, tag="bank")
                score_passes(acc[:, 0 : 2 * P], b, j, half * 2 * P)
                rows = work.tile([P, 2 * P], F32, tag="half_rows")
                copy(
                    out=rows[:].rearrange("p (r i) -> p r i", i=2),
                    in_=acc[:, 0 : 2 * P].rearrange("p (i r) -> p r i", i=2),
                )
                queue.dma_start(out=rows_of_group(b, j)[:, half * 2 * P : (half + 1) * 2 * P], in_=rows[:])

        V = nc.vector.tensor_copy
        A = nc.scalar.copy
        for c in range(2):
            for part in (IM, RE):
                transpose_weight("q", c, part)
            keep_warm(1)
        for part in (RE, IM):
            transpose_tokens(0, 0, part)
        keep_warm(1)
        for part in (RE, IM):
            transpose_tokens(0, 1, part)
        for c in range(2):
            negate_weight("q", c)
            if c == 0:
                quantise_weight("q", "im", c)
            quantise_weight("q", "re", c)
            quantise_weight("q", "im_neg", c)
        for part in (RE, IM):
            quantise_tokens(0, 0, part)
        quantise_weight("q", "im", 1)
        for c in range(2):
            for part in (IM, RE):
                split_weight("k", c, part, V)
        for part in (RE, IM):
            quantise_tokens(0, 1, part)
        project_queries(0)
        for c in range(2):
            for part in (IM, RE):
                transpose_weight("k", c, part)
        for half in range(2):
            for part in (RE, IM):
                split_tokens(1, half, part, A)
        project_queries(1)
        add_query_bias(0)
        for c in range(2):
            negate_weight("k", c)
            quantise_weight("k", "re", c)
            quantise_weight("k", "im_neg", c)
            if c == 0:
                project_queries(2)
        add_query_bias(1)
        project_all("k", 0, RE)
        add_query_bias(2)
        quantise_weight("k", "im", 0)
        quantise_weight("k", "im", 1)
        for j in range(3):
            quantise_queries(j)
        for half in range(2):
            for part in (RE, IM):
                transpose_tokens(1, half, part)
        project_all("k", 0, IM)
        for part in (RE, IM):
            quantise_tokens(1, 0, part)
        project_queries(3)
        interleave_all("k", 0, RE)
        for part in (RE, IM):
            quantise_tokens(1, 1, part)
        add_query_bias(3)
        project_all("k", 1, RE)
        quantise_all("k", 0, RE)
        interleave_all("k", 0, IM)
        quantise_queries(3)
        quantise_all("k", 0, IM)
        project_group(1, IM, 0)
        project_all("k", 1, IM)
        add_im_query_bias(0)
        interleave_all("k", 1, RE)
        project_group(1, IM, 1)
        score_rows(0, 0)
        add_im_query_bias(1)
        quantise_all("k", 1, RE)
        for pair in range(2):
            project_quarter(1, RE, pair, 0)
        for pair in range(2):
            project_quarter(1, RE, pair, 1)
        for pair in range(2):
            add_quarter_bias(1, RE, pair, 0)
        interleave_all("k", 1, IM)
        for pair in range(2):
            add_quarter_bias(1, RE, pair, 1)
        score_rows(0, 1)
        quantise_im_queries(0)
        quantise_all("k", 1, IM)
        interleave_half(1, RE, 0)
        project_group(1, IM, 2)
        score_rows(0, 2)
        interleave_half(1, RE, 1)
        quantise_half(1, RE, 0)
        add_im_query_bias(2)
        project_group(1, IM, 3)
        quantise_half(1, RE, 1)
        score_rows(0, 3)
        add_im_query_bias(3)
        quantise_im_queries(1)
        score_rows(1, 0)
        score_rows(1, 1)
        score_rows(1, 2)
        last_score_rows(1, 3)
